import numpy as np
import ml_dtypes


def mxq(x, axis, fmt="e4m3"):
    dtype, down = {"e4m3": (ml_dtypes.float8_e4m3fn, 7), "e5m2": (ml_dtypes.float8_e5m2, 14)}[fmt]
    v = np.moveaxis(np.asarray(x, np.float32).astype(ml_dtypes.bfloat16).astype(np.float64), axis, -1)
    blocks = v.reshape(v.shape[:-1] + (-1, 32))
    amax = np.abs(blocks).max(-1, keepdims=True)
    byte = np.maximum(np.where(amax > 0, np.frexp(amax)[1] - 1 + 127, 0) - down, 1)
    scale = np.exp2(byte - 127.0)
    codes = (blocks / scale).astype(np.float32).astype(dtype).astype(np.float64)
    return np.moveaxis((codes * scale).reshape(v.shape), -1, axis)


WIDE = False


def mx_kscale(k):
    if not WIDE:
        return np.ones(k)
    levels = np.array([10, -10, 5, -5, 0])
    if k % 512:
        return np.exp2(np.random.permutation(np.resize(levels, k // 32))).repeat(32)
    a = np.empty((k // 512, 16))
    for p in range(k // 512):
        a[p, :8] = np.random.permutation(np.resize(levels, 8))
        for g in range(8):
            far = levels[np.abs(levels - a[p, g]) >= 10]
            a[p, g + 8] = far[np.random.randint(len(far))]
    return np.exp2(a.ravel()).repeat(32)


BF16 = ml_dtypes.bfloat16


def bf(x):
    return np.asarray(x, np.float32).astype(BF16)


def f64(x):
    return np.asarray(x).astype(np.float64)


B, H, S, T, D = 2, 4, 1024, 1024, 128
DEGREE = 2
EPS = 1e-4


def setup_inputs():
    c = np.exp2(np.round(np.log2(mx_kscale(T)) / 2))
    g = 1.0 / np.sqrt(np.mean(c * c))
    u = np.random.uniform(0.1, 1.5, (B, H, S, 1))
    r = np.where(np.random.random((B, H, S, 1)) < 0.5, np.sqrt(EPS * u / T), 1.0)
    return {"q": bf(np.random.standard_normal((B, H, S, D)) * D ** -0.25 * r * g),
            "k": bf(np.random.standard_normal((B, H, T, D)) * D ** -0.25 * c[:, None]),
            "v": bf(np.random.standard_normal((B, H, T, D)) * 0.3 * np.sqrt(T) / (g * g * c * c)[:, None])}


def reference(q, k, v):
    dots = f64(q) @ f64(k).transpose(0, 1, 3, 2)
    x = dots ** DEGREE
    denom = np.maximum(x.sum(axis=-1, keepdims=True), EPS)
    attn = x / denom
    return mxq(attn, 3, "e4m3") @ mxq(f64(v), 2, "e4m3")

@@ -1,0 +1,285 @@
+from contextlib import ExitStack
+
+import concourse.mybir as mybir
+from concourse.masks import make_identity
+
+F32 = mybir.dt.float32
+BF16 = mybir.dt.bfloat16
+U32 = mybir.dt.uint32
+U8 = mybir.dt.uint8
+FP8X4 = mybir.dt.float8_e4m3fn_x4
+SQUARE = mybir.ActivationFunctionType.Square
+ADD = mybir.AluOpType.add
+MAX = mybir.AluOpType.max
+MULT = mybir.AluOpType.mult
+
+P = 128
+HEADS = 8
+S = 1024
+T = 1024
+D = 128
+EPS = 1e-4
+
+ROW_TILES = S // P
+N_TILES = HEADS * ROW_TILES
+BANK = 512
+HALVES = T // BANK
+PACK = 4
+K_PASS = P * PACK
+PASSES = T // K_PASS
+PAIRS = 2
+OUT_GROUP = BANK // D
+
+SUM_LAG = 1
+NORM_LAG = 2
+FLIP_LAG = 3
+EVAC_LAG = 4
+QUANT_LAG = 5
+PV_LAG = 6
+STORE_LAG = 7
+
+PREPARE_K_AT = 2
+PREPARE_Q_AT = 4
+
+V_AHEAD = 3
+
+
+FLOPS = 2 * 2 * HEADS * S * T * D
+
+
+def tile_polynomialattn_kernel(tc, q, k, v, out):
+    nc = tc.nc
+    q_heads = q.rearrange("b h s d -> (b h) s d")
+    k_heads = k.rearrange("b h t d -> (b h) t d")
+    v_heads = v.rearrange("b h t d -> (b h) t d")
+    out_heads = out.rearrange("b h s d -> (b h) s d")
+
+    with ExitStack() as ctx:
+        consts = ctx.enter_context(tc.tile_pool(name="consts", bufs=1))
+        inputs = ctx.enter_context(tc.tile_pool(name="inputs", bufs=1))
+        heads = ctx.enter_context(tc.tile_pool(name="heads", bufs=3))
+        work = ctx.enter_context(tc.tile_pool(name="work", bufs=3))
+        dots_ps = ctx.enter_context(tc.psum_pool(name="dots_ps", bufs=4))
+        flip_ps = ctx.enter_context(tc.psum_pool(name="flip_ps", bufs=3))
+        acc_ps = ctx.enter_context(tc.psum_pool(name="acc_ps", bufs=1))
+        ctx.enter_context(tc.manual_schedule())
+
+        q_in, k_in, v_in = {}, {}, {}
+
+        def load_qk(h):
+            k_in[h] = inputs.tile([P, ROW_TILES, D], BF16, name="k_in%d" % h)
+            nc.sync.dma_start(out=k_in[h][:], in_=k_heads[h].rearrange("(r p) d -> p r d", p=P))
+            q_in[h] = inputs.tile([P, ROW_TILES, D], BF16, name="q_in%d" % h)
+            nc.sync.dma_start(out=q_in[h][:], in_=q_heads[h].rearrange("(p r) d -> p r d", r=ROW_TILES))
+
+        def load_v(h):
+            v_in[h] = inputs.tile([P, PASSES * PACK, D], BF16, name="v_in%d" % h)
+            nc.sync.dma_start(
+                out=v_in[h][:].rearrange("p (g j) d -> p g j d", j=PACK),
+                in_=v_heads[h].rearrange("(g p j) d -> p g j d", p=P, j=PACK),
+            )
+
+        load_qk(0)
+        for h in range(V_AHEAD):
+            load_v(h)
+        for h in range(1, HEADS):
+            load_qk(h)
+            if h + V_AHEAD - 1 < HEADS:
+                load_v(h + V_AHEAD - 1)
+
+        ident_bf = consts.tile([P, P], BF16, name="ident_bf")
+        make_identity(nc, ident_bf[:])
+        ident_f32 = consts.tile([P, P], F32, name="ident_f32")
+        make_identity(nc, ident_f32[:])
+
+        qT, kT, v_grouped, v_codes, v_scales = {}, {}, {}, {}, {}
+        dots, x, rowsum, denom, rden, attn = {}, {}, {}, {}, {}, {}
+        flipped, grouped, codes, scales, acc = {}, {}, {}, {}, {}
+
+        def is_tile(i):
+            return 0 <= i < N_TILES
+
+        def flip_rows(rows):
+            bank = flip_ps.tile([P, ROW_TILES, P], BF16, name="flip_rows", tag="flip")
+            for r in range(ROW_TILES):
+                nc.tensor.transpose(out=bank[:, r, :], in_=rows[:, r, :], identity=ident_bf[:])
+            return bank
+
+        def keep_rows(bank, name):
+            turned = heads.tile([P, ROW_TILES * P], BF16, name=name)
+            words = bank[:].rearrange("d r p -> d (r p)").bitcast(F32)
+            nc.scalar.copy(out=turned[:].bitcast(F32), in_=words)
+            return turned
+
+        def keep_keys(bank):
+            turned = heads.tile([P, T], BF16, name="kT")
+            words = bank[:].rearrange("d r p -> d (r p)").bitcast(F32)
+            nc.scalar.copy(
+                out=turned[:].bitcast(F32).rearrange("d (g u p) -> d g u p", g=PASSES, u=PAIRS),
+                in_=words.rearrange("d (g p u) -> d g u p", g=PASSES, u=PAIRS),
+            )
+            return turned
+
+        def regroup_v(h):
+            v_grouped[h] = heads.tile([P, PASSES, D, PACK], BF16, name="v_grouped", align_bytes=64)
+            nc.vector.tensor_copy(
+                out=v_grouped[h][:], in_=v_in[h][:].rearrange("p (g j) d -> p g d j", j=PACK)
+            )
+
+        def quantise_v(h):
+            v_codes[h] = inputs.tile([P, PASSES * D], U32, name="v_codes%d" % h, align_bytes=64)
+            v_scales[h] = inputs.tile([P, PASSES * D], U8, name="v_scales%d" % h, align_bytes=64)
+            nc.vector.quantize_mx(
+                out=v_codes[h][:].bitcast(FP8X4),
+                scales=v_scales[h][:],
+                in_=v_grouped[h][:].rearrange("p g d j -> p (g d j)"),
+            )
+
+        def score_matmul(i, half):
+            h, r = divmod(i, ROW_TILES)
+            dots[i, half] = dots_ps.tile([P, BANK], F32, name="dots")
+            nc.tensor.matmul(
+                out=dots[i, half][:],
+                lhsT=qT[h][:, r * P : (r + 1) * P],
+                rhs=kT[h][:, half * BANK : (half + 1) * BANK],
+                start=True,
+                stop=True,
+            )
+
+        def square(i, half):
+            if half == 0:
+                x[i] = work.tile([P, T], F32, name="x", bufs=4)
+                rowsum[i] = work.tile([P, HALVES], F32, name="rowsum")
+            nc.scalar.activation(
+                out=x[i][:, half * BANK : (half + 1) * BANK],
+                in_=dots[i, half][:],
+                func=SQUARE,
+                accum_out=rowsum[i][:, half : half + 1],
+            )
+
+        def clamp_sum(i):
+            denom[i] = work.tile([P, 1], F32, name="denom")
+            nc.vector.tensor_scalar(
+                out=denom[i][:],
+                in0=rowsum[i][:, 0:1],
+                scalar1=rowsum[i][:, 1:2],
+                scalar2=EPS,
+                op0=ADD,
+                op1=MAX,
+            )
+
+        def invert(i):
+            rden[i] = work.tile([P, 1], F32, name="rden")
+            nc.vector.reciprocal(out=rden[i][:], in_=denom[i][:])
+
+        def normalise(i):
+            attn[i] = work.tile([P, T], BF16, name="attn")
+            nc.vector.tensor_scalar(
+                out=attn[i][:], in0=x[i][:], scalar1=rden[i][:, 0:1], scalar2=None, op0=MULT
+            )
+
+        def flip_words(i, g):
+            if g == 0:
+                flipped[i] = flip_ps.tile([P, PASSES * PAIRS, P], F32, name="flipped", tag="flip")
+            words = attn[i][:].bitcast(F32)
+            for u in range(PAIRS):
+                c = PAIRS * g + u
+                nc.tensor.transpose(
+                    out=flipped[i][:, c, :], in_=words[:, c * P : (c + 1) * P], identity=ident_f32[:]
+                )
+
+        def on_scalar(i):
+            return i % ROW_TILES == 0 or i + EVAC_LAG >= N_TILES
+
+        def evacuate(i):
+            grouped[i] = work.tile([P, PASSES * P * PACK], BF16, name="grouped", align_bytes=64)
+            dst = grouped[i][:].bitcast(F32).rearrange("p (g s u) -> p g s u", g=PASSES, u=PAIRS)
+            src = flipped[i][:].rearrange("p (g u) s -> p g s u", u=PAIRS)
+            if on_scalar(i):
+                nc.scalar.copy(out=dst, in_=src)
+            else:
+                nc.vector.tensor_copy(out=dst, in_=src)
+
+        def quantise(i):
+            codes[i] = work.tile([P, PASSES * P], U32, name="codes", align_bytes=64)
+            scales[i] = work.tile([P, PASSES * P], U8, name="scales", align_bytes=64)
+            nc.vector.quantize_mx(
+                out=codes[i][:].bitcast(FP8X4), scales=scales[i][:], in_=grouped[i][:]
+            )
+
+        def attn_times_v(i):
+            h, r = divmod(i, ROW_TILES)
+            first = i - i % OUT_GROUP
+            if i == first:
+                acc[first] = acc_ps.tile([P, OUT_GROUP, D], F32, name="acc")
+            for g in range(PASSES):
+                nc.tensor.matmul_mx(
+                    out=acc[first][:, i - first, :],
+                    lhsT=codes[i][:, g * P : (g + 1) * P].bitcast(FP8X4),
+                    lhsT_scale=scales[i][:, g * P : (g + 1) * P],
+                    rhs=v_codes[h][:, g * D : (g + 1) * D].bitcast(FP8X4),
+                    rhs_scale=v_scales[h][:, g * D : (g + 1) * D],
+                    start=(g == 0),
+                    stop=(g == PASSES - 1),
+                )
+
+        def store(last):
+            h, r = divmod(last, ROW_TILES)
+            result = work.tile([P, OUT_GROUP, D], F32, name="result")
+            nc.scalar.copy(out=result[:], in_=acc[last + 1 - OUT_GROUP][:])
+            rows = out_heads[h].rearrange("(p r) d -> p r d", r=ROW_TILES)
+            nc.sync.dma_start(out=rows[:, r + 1 - OUT_GROUP : r + 1, :], in_=result[:])
+
+        kT[0] = keep_keys(flip_rows(k_in[0]))
+        qT[0] = keep_rows(flip_rows(q_in[0]), "qT")
+        for h in range(V_AHEAD):
+            regroup_v(h)
+        for h in range(V_AHEAD):
+            quantise_v(h)
+
+        flipped_rows = {}
+        for it in range(-1, N_TILES + STORE_LAG + 1):
+            next_head = it // ROW_TILES + 1
+            at = it % ROW_TILES if is_tile(it) and next_head < HEADS else -1
+            v_head = it // ROW_TILES + V_AHEAD
+            v_at = it % ROW_TILES if is_tile(it) and v_head < HEADS else -1
+
+            if is_tile(it):
+                square(it, 0)
+            if at == PREPARE_K_AT + 1:
+                kT[next_head] = keep_keys(flipped_rows["k"])
+            if at == PREPARE_Q_AT + 1:
+                qT[next_head] = keep_rows(flipped_rows["q"], "qT")
+            if is_tile(it - STORE_LAG) and (it - STORE_LAG) % OUT_GROUP == OUT_GROUP - 1:
+                store(it - STORE_LAG)
+            if is_tile(it - EVAC_LAG) and on_scalar(it - EVAC_LAG):
+                evacuate(it - EVAC_LAG)
+            if is_tile(it):
+                square(it, 1)
+
+            for half in range(HALVES):
+                if is_tile(it + 1):
+                    score_matmul(it + 1, half)
+                if is_tile(it - FLIP_LAG):
+                    flip_words(it - FLIP_LAG, half)
+            if is_tile(it - PV_LAG):
+                attn_times_v(it - PV_LAG)
+            if at == PREPARE_K_AT:
+                flipped_rows["k"] = flip_rows(k_in[next_head])
+            if at == PREPARE_Q_AT:
+                flipped_rows["q"] = flip_rows(q_in[next_head])
+
+            if is_tile(it - NORM_LAG):
+                normalise(it - NORM_LAG)
+            if is_tile(it - SUM_LAG):
+                clamp_sum(it - SUM_LAG)
+            if v_at == PREPARE_K_AT:
+                regroup_v(v_head)
+            if v_at == PREPARE_Q_AT:
+                quantise_v(v_head)
+            if is_tile(it - QUANT_LAG):
+                quantise(it - QUANT_LAG)
+            if is_tile(it - SUM_LAG):
+                invert(it - SUM_LAG)
+            if is_tile(it - EVAC_LAG) and not on_scalar(it - EVAC_LAG):
+                evacuate(it - EVAC_LAG)

@@ -30,13 +30,13 @@ PASSES = T // K_PASS
 PAIRS = 2
 OUT_GROUP = BANK // D
 
-SUM_LAG = 1
-NORM_LAG = 2
-FLIP_LAG = 3
-EVAC_LAG = 4
-QUANT_LAG = 5
-PV_LAG = 6
-STORE_LAG = 7
+SUM_LAG = 2
+NORM_LAG = 3
+FLIP_LAG = 5
+EVAC_LAG = 6
+QUANT_LAG = 7
+PV_LAG = 8
+STORE_LAG = 9
 
 PREPARE_K_AT = 2
 PREPARE_Q_AT = 4
@@ -148,8 +148,8 @@ def tile_polynomialattn_kernel(tc, q, k, v, out):
 
         def square(i, half):
             if half == 0:
-                x[i] = work.tile([P, T], F32, name="x", bufs=4)
-                rowsum[i] = work.tile([P, HALVES], F32, name="rowsum")
+                x[i] = work.tile([P, T], F32, name="x", bufs=5)
+                rowsum[i] = work.tile([P, HALVES], F32, name="rowsum", bufs=5)
             nc.scalar.activation(
                 out=x[i][:, half * BANK : (half + 1) * BANK],
                 in_=dots[i, half][:],
@@ -173,7 +173,7 @@ def tile_polynomialattn_kernel(tc, q, k, v, out):
             nc.vector.reciprocal(out=rden[i][:], in_=denom[i][:])
 
         def normalise(i):
-            attn[i] = work.tile([P, T], BF16, name="attn")
+            attn[i] = work.tile([P, T], BF16, name="attn", bufs=4)
             nc.vector.tensor_scalar(
                 out=attn[i][:], in0=x[i][:], scalar1=rden[i][:, 0:1], scalar2=None, op0=MULT
             )
@@ -201,8 +201,8 @@ def tile_polynomialattn_kernel(tc, q, k, v, out):
                 nc.vector.tensor_copy(out=dst, in_=src)
 
         def quantise(i):
-            codes[i] = work.tile([P, PASSES * P], U32, name="codes", align_bytes=64)
-            scales[i] = work.tile([P, PASSES * P], U8, name="scales", align_bytes=64)
+            codes[i] = work.tile([P, PASSES * P], U32, name="codes", align_bytes=64, bufs=4)
+            scales[i] = work.tile([P, PASSES * P], U8, name="scales", align_bytes=64, bufs=4)
             nc.vector.quantize_mx(
                 out=codes[i][:].bitcast(FP8X4), scales=scales[i][:], in_=grouped[i][:]
             )
@@ -229,6 +229,10 @@ def tile_polynomialattn_kernel(tc, q, k, v, out):
             nc.scalar.copy(out=result[:], in_=acc[last + 1 - OUT_GROUP][:])
             rows = out_heads[h].rearrange("(p r) d -> p r d", r=ROW_TILES)
             nc.sync.dma_start(out=rows[:, r + 1 - OUT_GROUP : r + 1, :], in_=result[:])
+
+        def multiplied_in(it):
+            tiles = [it - PV_LAG - 1, it - PV_LAG]
+            return [i for i in tiles if is_tile(i) and (i % OUT_GROUP == 0) == (i == tiles[0])]
 
         kT[0] = keep_keys(flip_rows(k_in[0]))
         qT[0] = keep_rows(flip_rows(q_in[0]), "qT")
@@ -262,8 +266,8 @@ def tile_polynomialattn_kernel(tc, q, k, v, out):
                     score_matmul(it + 1, half)
                 if is_tile(it - FLIP_LAG):
                     flip_words(it - FLIP_LAG, half)
-            if is_tile(it - PV_LAG):
-                attn_times_v(it - PV_LAG)
+            for i in multiplied_in(it):
+                attn_times_v(i)
             if at == PREPARE_K_AT:
                 flipped_rows["k"] = flip_rows(k_in[next_head])
             if at == PREPARE_Q_AT:

@@ -29,19 +29,21 @@ K_PASS = P * PACK
 PASSES = T // K_PASS
 PAIRS = 2
 OUT_GROUP = BANK // D
+SUM_GROUP = 4
 
-SUM_LAG = 2
-NORM_LAG = 3
-FLIP_LAG = 5
-EVAC_LAG = 6
-QUANT_LAG = 7
-PV_LAG = 8
-STORE_LAG = 9
+NORM_LAG = SUM_GROUP + 1
+FLIP_LAG = NORM_LAG + 1
+EVAC_LAG = FLIP_LAG + 1
+QUANT_LAG = EVAC_LAG + 1
+PV_LAG = QUANT_LAG + 1
+STORE_LAG = PV_LAG + 1
 
 PREPARE_K_AT = 2
-PREPARE_Q_AT = 4
+PREPARE_Q_AT = 5
 
-V_AHEAD = 3
+SCALAR_EVERY = 12
+
+EARLY_HEADS = 2
 
 
 FLOPS = 2 * 2 * HEADS * S * T * D
@@ -66,11 +68,15 @@ def tile_polynomialattn_kernel(tc, q, k, v, out):
 
         q_in, k_in, v_in = {}, {}, {}
 
-        def load_qk(h):
+        def load_qk(h, pieces):
             k_in[h] = inputs.tile([P, ROW_TILES, D], BF16, name="k_in%d" % h)
-            nc.sync.dma_start(out=k_in[h][:], in_=k_heads[h].rearrange("(r p) d -> p r d", p=P))
             q_in[h] = inputs.tile([P, ROW_TILES, D], BF16, name="q_in%d" % h)
-            nc.sync.dma_start(out=q_in[h][:], in_=q_heads[h].rearrange("(p r) d -> p r d", r=ROW_TILES))
+            k_rows = k_heads[h].rearrange("(r p) d -> p r d", p=P)
+            q_rows = q_heads[h].rearrange("(p r) d -> p r d", r=ROW_TILES)
+            for i in range(pieces):
+                blocks = slice(i * ROW_TILES // pieces, (i + 1) * ROW_TILES // pieces)
+                nc.sync.dma_start(out=k_in[h][:, blocks, :], in_=k_rows[:, blocks, :])
+                nc.sync.dma_start(out=q_in[h][:, blocks, :], in_=q_rows[:, blocks, :])
 
         def load_v(h):
             v_in[h] = inputs.tile([P, PASSES * PACK, D], BF16, name="v_in%d" % h)
@@ -79,13 +85,15 @@ def tile_polynomialattn_kernel(tc, q, k, v, out):
                 in_=v_heads[h].rearrange("(g p j) d -> p g j d", p=P, j=PACK),
             )
 
-        load_qk(0)
-        for h in range(V_AHEAD):
+        load_qk(0, HALVES)
+        for h in range(EARLY_HEADS):
             load_v(h)
-        for h in range(1, HEADS):
-            load_qk(h)
-            if h + V_AHEAD - 1 < HEADS:
-                load_v(h + V_AHEAD - 1)
+        for h in range(1, EARLY_HEADS):
+            load_qk(h, 1)
+        for h in range(EARLY_HEADS, HEADS):
+            load_v(h)
+        for h in range(EARLY_HEADS, HEADS):
+            load_qk(h, 1)
 
         ident_bf = consts.tile([P, P], BF16, name="ident_bf")
         make_identity(nc, ident_bf[:])
@@ -99,26 +107,29 @@ def tile_polynomialattn_kernel(tc, q, k, v, out):
         def is_tile(i):
             return 0 <= i < N_TILES
 
-        def flip_rows(rows):
+        def flip_rows(rows, blocks):
             bank = flip_ps.tile([P, ROW_TILES, P], BF16, name="flip_rows", tag="flip")
-            for r in range(ROW_TILES):
+            for r in blocks:
                 nc.tensor.transpose(out=bank[:, r, :], in_=rows[:, r, :], identity=ident_bf[:])
             return bank
 
-        def keep_rows(bank, name):
-            turned = heads.tile([P, ROW_TILES * P], BF16, name=name)
-            words = bank[:].rearrange("d r p -> d (r p)").bitcast(F32)
-            nc.scalar.copy(out=turned[:].bitcast(F32), in_=words)
-            return turned
+        def words_of(tile, blocks):
+            width = P // 2
+            return tile.bitcast(F32)[:, blocks[0] * width : (blocks[-1] + 1) * width]
 
-        def keep_keys(bank):
-            turned = heads.tile([P, T], BF16, name="kT")
-            words = bank[:].rearrange("d r p -> d (r p)").bitcast(F32)
-            nc.scalar.copy(
-                out=turned[:].bitcast(F32).rearrange("d (g u p) -> d g u p", g=PASSES, u=PAIRS),
-                in_=words.rearrange("d (g p u) -> d g u p", g=PASSES, u=PAIRS),
+        def keep_queries(copy, bank, turned, blocks):
+            flat = bank[:].rearrange("d r p -> d (r p)")
+            copy(out=words_of(turned[:], blocks), in_=words_of(flat, blocks))
+
+        def keep_keys(copy, bank, turned, blocks):
+            flat = bank[:].rearrange("d r p -> d (r p)")
+            copy(
+                out=words_of(turned[:], blocks).rearrange("d (g u p) -> d g u p", u=PAIRS, p=P),
+                in_=words_of(flat, blocks).rearrange("d (g p u) -> d g u p", u=PAIRS, p=P),
             )
-            return turned
+
+        def new_turned(name):
+            return heads.tile([P, ROW_TILES * P], BF16, name=name)
 
         def regroup_v(h):
             v_grouped[h] = heads.tile([P, PASSES, D, PACK], BF16, name="v_grouped", align_bytes=64)
@@ -147,35 +158,38 @@ def tile_polynomialattn_kernel(tc, q, k, v, out):
             )
 
         def square(i, half):
+            m, j = divmod(i, SUM_GROUP)
             if half == 0:
-                x[i] = work.tile([P, T], F32, name="x", bufs=5)
-                rowsum[i] = work.tile([P, HALVES], F32, name="rowsum", bufs=5)
+                x[i] = work.tile([P, T], F32, name="x", bufs=NORM_LAG + 2)
+            if half == 0 and j == 0:
+                rowsum[m] = work.tile([P, SUM_GROUP, HALVES], F32, name="rowsum")
             nc.scalar.activation(
                 out=x[i][:, half * BANK : (half + 1) * BANK],
                 in_=dots[i, half][:],
                 func=SQUARE,
-                accum_out=rowsum[i][:, half : half + 1],
+                accum_out=rowsum[m][:, j, half : half + 1],
             )
 
-        def clamp_sum(i):
-            denom[i] = work.tile([P, 1], F32, name="denom")
+        def add_sums(m):
+            denom[m] = work.tile([P, SUM_GROUP], F32, name="denom")
+            nc.vector.tensor_tensor(
+                out=denom[m][:], in0=rowsum[m][:, :, 0], in1=rowsum[m][:, :, 1], op=ADD
+            )
+
+        def clamp(m):
             nc.vector.tensor_scalar(
-                out=denom[i][:],
-                in0=rowsum[i][:, 0:1],
-                scalar1=rowsum[i][:, 1:2],
-                scalar2=EPS,
-                op0=ADD,
-                op1=MAX,
+                out=denom[m][:], in0=denom[m][:], scalar1=EPS, scalar2=None, op0=MAX
             )
 
-        def invert(i):
-            rden[i] = work.tile([P, 1], F32, name="rden")
-            nc.vector.reciprocal(out=rden[i][:], in_=denom[i][:])
+        def invert(m):
+            rden[m] = work.tile([P, SUM_GROUP], F32, name="rden")
+            nc.vector.reciprocal(out=rden[m][:], in_=denom[m][:])
 
         def normalise(i):
-            attn[i] = work.tile([P, T], BF16, name="attn", bufs=4)
+            m, j = divmod(i, SUM_GROUP)
+            attn[i] = work.tile([P, T], BF16, name="attn")
             nc.vector.tensor_scalar(
-                out=attn[i][:], in0=x[i][:], scalar1=rden[i][:, 0:1], scalar2=None, op0=MULT
+                out=attn[i][:], in0=x[i][:], scalar1=rden[m][:, j : j + 1], scalar2=None, op0=MULT
             )
 
         def flip_words(i, g):
@@ -189,7 +203,7 @@ def tile_polynomialattn_kernel(tc, q, k, v, out):
                 )
 
         def on_scalar(i):
-            return i % ROW_TILES == 0 or i + EVAC_LAG >= N_TILES
+            return i % SCALAR_EVERY == 0 or i + EVAC_LAG >= N_TILES
 
         def evacuate(i):
             grouped[i] = work.tile([P, PASSES * P * PACK], BF16, name="grouped", align_bytes=64)
@@ -223,39 +237,55 @@ def tile_polynomialattn_kernel(tc, q, k, v, out):
                     stop=(g == PASSES - 1),
                 )
 
-        def store(last):
-            h, r = divmod(last, ROW_TILES)
-            result = work.tile([P, OUT_GROUP, D], F32, name="result")
-            nc.scalar.copy(out=result[:], in_=acc[last + 1 - OUT_GROUP][:])
-            rows = out_heads[h].rearrange("(p r) d -> p r d", r=ROW_TILES)
-            nc.sync.dma_start(out=rows[:, r + 1 - OUT_GROUP : r + 1, :], in_=result[:])
-
         def multiplied_in(it):
             tiles = [it - PV_LAG - 1, it - PV_LAG]
             return [i for i in tiles if is_tile(i) and (i % OUT_GROUP == 0) == (i == tiles[0])]
 
-        kT[0] = keep_keys(flip_rows(k_in[0]))
-        qT[0] = keep_rows(flip_rows(q_in[0]), "qT")
-        for h in range(V_AHEAD):
-            regroup_v(h)
-        for h in range(V_AHEAD):
-            quantise_v(h)
+        def store(last, count):
+            h, r = divmod(last, ROW_TILES)
+            bank = acc[last - last % OUT_GROUP]
+            end = last % OUT_GROUP + 1
+            result = work.tile([P, OUT_GROUP, D], F32, name="result")
+            nc.scalar.copy(out=result[:, :count, :], in_=bank[:, end - count : end, :])
+            rows = out_heads[h].rearrange("(p r) d -> p r d", r=ROW_TILES)
+            nc.sync.dma_start(out=rows[:, r + 1 - count : r + 1, :], in_=result[:, :count, :])
+
+        kT[0], qT[0] = new_turned("kT"), new_turned("qT")
+        for half in range(HALVES):
+            blocks = range(half * ROW_TILES // HALVES, (half + 1) * ROW_TILES // HALVES)
+            keep_keys(nc.scalar.copy, flip_rows(k_in[0], blocks), kT[0], blocks)
+            keep_queries(nc.vector.tensor_copy, flip_rows(q_in[0], blocks), qT[0], blocks)
+
+        for h in range(HEADS + 1):
+            if h < HEADS:
+                regroup_v(h)
+            if h >= 1:
+                quantise_v(h - 1)
 
         flipped_rows = {}
+        all_blocks = range(ROW_TILES)
         for it in range(-1, N_TILES + STORE_LAG + 1):
             next_head = it // ROW_TILES + 1
             at = it % ROW_TILES if is_tile(it) and next_head < HEADS else -1
-            v_head = it // ROW_TILES + V_AHEAD
-            v_at = it % ROW_TILES if is_tile(it) and v_head < HEADS else -1
+            m = it // SUM_GROUP - 1 if it % SUM_GROUP == 0 and 0 < it <= N_TILES else -1
+            stored = it - STORE_LAG
 
             if is_tile(it):
                 square(it, 0)
             if at == PREPARE_K_AT + 1:
-                kT[next_head] = keep_keys(flipped_rows["k"])
+                kT[next_head] = new_turned("kT")
+                keep_keys(nc.scalar.copy, flipped_rows["k"], kT[next_head], all_blocks)
             if at == PREPARE_Q_AT + 1:
-                qT[next_head] = keep_rows(flipped_rows["q"], "qT")
-            if is_tile(it - STORE_LAG) and (it - STORE_LAG) % OUT_GROUP == OUT_GROUP - 1:
-                store(it - STORE_LAG)
+                qT[next_head] = new_turned("qT")
+                keep_queries(nc.scalar.copy, flipped_rows["q"], qT[next_head], all_blocks)
+            if is_tile(stored):
+                if stored >= N_TILES - OUT_GROUP:
+                    if stored == N_TILES - 2:
+                        store(stored, OUT_GROUP - 1)
+                    if stored == N_TILES - 1:
+                        store(stored, 1)
+                elif stored % OUT_GROUP == OUT_GROUP - 1:
+                    store(stored, OUT_GROUP)
             if is_tile(it - EVAC_LAG) and on_scalar(it - EVAC_LAG):
                 evacuate(it - EVAC_LAG)
             if is_tile(it):
@@ -269,21 +299,19 @@ def tile_polynomialattn_kernel(tc, q, k, v, out):
             for i in multiplied_in(it):
                 attn_times_v(i)
             if at == PREPARE_K_AT:
-                flipped_rows["k"] = flip_rows(k_in[next_head])
+                flipped_rows["k"] = flip_rows(k_in[next_head], all_blocks)
             if at == PREPARE_Q_AT:
-                flipped_rows["q"] = flip_rows(q_in[next_head])
+                flipped_rows["q"] = flip_rows(q_in[next_head], all_blocks)
 
             if is_tile(it - NORM_LAG):
                 normalise(it - NORM_LAG)
-            if is_tile(it - SUM_LAG):
-                clamp_sum(it - SUM_LAG)
-            if v_at == PREPARE_K_AT:
-                regroup_v(v_head)
-            if v_at == PREPARE_Q_AT:
-                quantise_v(v_head)
+            if m >= 0:
+                add_sums(m)
             if is_tile(it - QUANT_LAG):
                 quantise(it - QUANT_LAG)
-            if is_tile(it - SUM_LAG):
-                invert(it - SUM_LAG)
+            if m >= 0:
+                clamp(m)
             if is_tile(it - EVAC_LAG) and not on_scalar(it - EVAC_LAG):
                 evacuate(it - EVAC_LAG)
+            if m >= 0:
+                invert(m)

@@ -294,6 +294,7 @@ def tile_polynomialattn_kernel(tc, q, k, v, out):
             for half in range(HALVES):
                 if is_tile(it + 1):
                     score_matmul(it + 1, half)
+            for half in range(HALVES):
                 if is_tile(it - FLIP_LAG):
                     flip_words(it - FLIP_LAG, half)
             for i in multiplied_in(it):

@@ -41,8 +41,6 @@ STORE_LAG = PV_LAG + 1
 PREPARE_K_AT = 2
 PREPARE_Q_AT = 5
 
-SCALAR_EVERY = 12
-
 EARLY_HEADS = 2
 
 
@@ -160,9 +158,9 @@ def tile_polynomialattn_kernel(tc, q, k, v, out):
         def square(i, half):
             m, j = divmod(i, SUM_GROUP)
             if half == 0:
-                x[i] = work.tile([P, T], F32, name="x", bufs=NORM_LAG + 2)
+                x[i] = work.tile([P, T], F32, name="x", bufs=NORM_LAG + 6)
             if half == 0 and j == 0:
-                rowsum[m] = work.tile([P, SUM_GROUP, HALVES], F32, name="rowsum")
+                rowsum[m] = work.tile([P, SUM_GROUP, HALVES], F32, name="rowsum", bufs=5)
             nc.scalar.activation(
                 out=x[i][:, half * BANK : (half + 1) * BANK],
                 in_=dots[i, half][:],
@@ -203,7 +201,7 @@ def tile_polynomialattn_kernel(tc, q, k, v, out):
                 )
 
         def on_scalar(i):
-            return i % SCALAR_EVERY == 0 or i + EVAC_LAG >= N_TILES
+            return i + EVAC_LAG >= N_TILES
 
         def evacuate(i):
             grouped[i] = work.tile([P, PASSES * P * PACK], BF16, name="grouped", align_bytes=64)
@@ -297,19 +295,21 @@ def tile_polynomialattn_kernel(tc, q, k, v, out):
             for half in range(HALVES):
                 if is_tile(it - FLIP_LAG):
                     flip_words(it - FLIP_LAG, half)
-            for i in multiplied_in(it):
-                attn_times_v(i)
             if at == PREPARE_K_AT:
                 flipped_rows["k"] = flip_rows(k_in[next_head], all_blocks)
             if at == PREPARE_Q_AT:
                 flipped_rows["q"] = flip_rows(q_in[next_head], all_blocks)
+            for i in multiplied_in(it):
+                attn_times_v(i)
 
-            if is_tile(it - NORM_LAG):
-                normalise(it - NORM_LAG)
-            if m >= 0:
-                add_sums(m)
-            if is_tile(it - QUANT_LAG):
-                quantise(it - QUANT_LAG)
+            steps = [(normalise, it - NORM_LAG), (quantise, it - QUANT_LAG)]
+            if it % SUM_GROUP == 1:
+                steps.reverse()
+            for n, (step, i) in enumerate(steps):
+                if is_tile(i):
+                    step(i)
+                if m >= 0 and n == 0:
+                    add_sums(m)
             if m >= 0:
                 clamp(m)
             if is_tile(it - EVAC_LAG) and not on_scalar(it - EVAC_LAG):

@@ -41,7 +41,13 @@ STORE_LAG = PV_LAG + 1
 PREPARE_K_AT = 2
 PREPARE_Q_AT = 5
 
-EARLY_HEADS = 2
+SCALAR_TILE = 3
+
+EARLY_HEADS = [1]
+
+V_AHEAD = 2
+REGROUP_V_AT = 3
+QUANTISE_V_AT = 7
 
 
 FLOPS = 2 * 2 * HEADS * S * T * D
@@ -84,14 +90,14 @@ def tile_polynomialattn_kernel(tc, q, k, v, out):
             )
 
         load_qk(0, HALVES)
-        for h in range(EARLY_HEADS):
+        load_v(0)
+        load_qk(1, 1)
+        load_v(1)
+        load_qk(2, 1)
+        for h in range(2, HEADS):
             load_v(h)
-        for h in range(1, EARLY_HEADS):
-            load_qk(h, 1)
-        for h in range(EARLY_HEADS, HEADS):
-            load_v(h)
-        for h in range(EARLY_HEADS, HEADS):
-            load_qk(h, 1)
+            if h + 1 < HEADS:
+                load_qk(h + 1, 1)
 
         ident_bf = consts.tile([P, P], BF16, name="ident_bf")
         make_identity(nc, ident_bf[:])
@@ -201,7 +207,7 @@ def tile_polynomialattn_kernel(tc, q, k, v, out):
                 )
 
         def on_scalar(i):
-            return i + EVAC_LAG >= N_TILES
+            return i % ROW_TILES == SCALAR_TILE or i + EVAC_LAG >= N_TILES
 
         def evacuate(i):
             grouped[i] = work.tile([P, PASSES * P * PACK], BF16, name="grouped", align_bytes=64)
@@ -254,17 +260,20 @@ def tile_polynomialattn_kernel(tc, q, k, v, out):
             keep_keys(nc.scalar.copy, flip_rows(k_in[0], blocks), kT[0], blocks)
             keep_queries(nc.vector.tensor_copy, flip_rows(q_in[0], blocks), qT[0], blocks)
 
-        for h in range(HEADS + 1):
-            if h < HEADS:
-                regroup_v(h)
-            if h >= 1:
-                quantise_v(h - 1)
+        for h in range(V_AHEAD):
+            regroup_v(h)
+        for h in range(V_AHEAD):
+            quantise_v(h)
 
         flipped_rows = {}
         all_blocks = range(ROW_TILES)
         for it in range(-1, N_TILES + STORE_LAG + 1):
             next_head = it // ROW_TILES + 1
             at = it % ROW_TILES if is_tile(it) and next_head < HEADS else -1
+            if next_head in EARLY_HEADS:
+                at = -1
+            v_head = it // ROW_TILES + V_AHEAD
+            v_at = it % ROW_TILES if is_tile(it) and v_head < HEADS else -1
             m = it // SUM_GROUP - 1 if it % SUM_GROUP == 0 and 0 < it <= N_TILES else -1
             stored = it - STORE_LAG
 
@@ -295,6 +304,9 @@ def tile_polynomialattn_kernel(tc, q, k, v, out):
             for half in range(HALVES):
                 if is_tile(it - FLIP_LAG):
                     flip_words(it - FLIP_LAG, half)
+            if 0 <= it < 2 * len(EARLY_HEADS):
+                rows = k_in if it % 2 == 0 else q_in
+                flipped_rows[it] = flip_rows(rows[EARLY_HEADS[it // 2]], all_blocks)
             if at == PREPARE_K_AT:
                 flipped_rows["k"] = flip_rows(k_in[next_head], all_blocks)
             if at == PREPARE_Q_AT:
@@ -312,6 +324,16 @@ def tile_polynomialattn_kernel(tc, q, k, v, out):
                     add_sums(m)
             if m >= 0:
                 clamp(m)
+            if v_at == REGROUP_V_AT:
+                regroup_v(v_head)
+            if v_at == QUANTISE_V_AT:
+                quantise_v(v_head)
+            early = it - 1
+            if early in flipped_rows:
+                h = EARLY_HEADS[early // 2]
+                turned, keep = (kT, keep_keys) if early % 2 == 0 else (qT, keep_queries)
+                turned[h] = new_turned("kT" if early % 2 == 0 else "qT")
+                keep(nc.vector.tensor_copy, flipped_rows[early], turned[h], all_blocks)
             if is_tile(it - EVAC_LAG) and not on_scalar(it - EVAC_LAG):
                 evacuate(it - EVAC_LAG)
             if m >= 0:

@@ -8,6 +8,7 @@ BF16 = mybir.dt.bfloat16
 U32 = mybir.dt.uint32
 U8 = mybir.dt.uint8
 FP8X4 = mybir.dt.float8_e4m3fn_x4
+COPY = mybir.ActivationFunctionType.Copy
 SQUARE = mybir.ActivationFunctionType.Square
 ADD = mybir.AluOpType.add
 MAX = mybir.AluOpType.max
@@ -43,11 +44,13 @@ PREPARE_Q_AT = 5
 
 SCALAR_TILE = 3
 
-EARLY_HEADS = [1]
+EARLY_HEADS = [1, 2]
+
+FIRST_SCORES = 2
 
 V_AHEAD = 2
 REGROUP_V_AT = 3
-QUANTISE_V_AT = 7
+QUANTISE_V_AT = 4
 
 
 FLOPS = 2 * 2 * HEADS * S * T * D
@@ -152,7 +155,7 @@ def tile_polynomialattn_kernel(tc, q, k, v, out):
 
         def score_matmul(i, half):
             h, r = divmod(i, ROW_TILES)
-            dots[i, half] = dots_ps.tile([P, BANK], F32, name="dots")
+            dots[i, half] = dots_ps.tile([P, BANK], F32, name="dots", tag="dots")
             nc.tensor.matmul(
                 out=dots[i, half][:],
                 lhsT=qT[h][:, r * P : (r + 1) * P],
@@ -189,12 +192,16 @@ def tile_polynomialattn_kernel(tc, q, k, v, out):
             rden[m] = work.tile([P, SUM_GROUP], F32, name="rden")
             nc.vector.reciprocal(out=rden[m][:], in_=denom[m][:])
 
-        def normalise(i):
+        def normalise(i, on_vector=True):
             m, j = divmod(i, SUM_GROUP)
-            attn[i] = work.tile([P, T], BF16, name="attn")
-            nc.vector.tensor_scalar(
-                out=attn[i][:], in0=x[i][:], scalar1=rden[m][:, j : j + 1], scalar2=None, op0=MULT
-            )
+            attn[i] = work.tile([P, T], BF16, name="attn", bufs=SUM_GROUP + 1)
+            factor = rden[m][:, j : j + 1]
+            if on_vector:
+                nc.vector.tensor_scalar(
+                    out=attn[i][:], in0=x[i][:], scalar1=factor, scalar2=None, op0=MULT
+                )
+            else:
+                nc.scalar.activation(out=attn[i][:], in_=x[i][:], func=COPY, scale=factor)
 
         def flip_words(i, g):
             if g == 0:
@@ -206,7 +213,13 @@ def tile_polynomialattn_kernel(tc, q, k, v, out):
                     out=flipped[i][:, c, :], in_=words[:, c * P : (c + 1) * P], identity=ident_f32[:]
                 )
 
+        def flip(i):
+            for g in range(PASSES):
+                flip_words(i, g)
+
         def on_scalar(i):
+            if i == N_TILES - 2:
+                return False
             return i % ROW_TILES == SCALAR_TILE or i + EVAC_LAG >= N_TILES
 
         def evacuate(i):
@@ -225,10 +238,15 @@ def tile_polynomialattn_kernel(tc, q, k, v, out):
                 out=codes[i][:].bitcast(FP8X4), scales=scales[i][:], in_=grouped[i][:]
             )
 
+        def first_in_bank(i):
+            return i if i == N_TILES - 1 else i - i % OUT_GROUP
+
         def attn_times_v(i):
             h, r = divmod(i, ROW_TILES)
-            first = i - i % OUT_GROUP
-            if i == first:
+            first = first_in_bank(i)
+            if i == first and i >= N_TILES - OUT_GROUP:
+                acc[first] = dots_ps.tile([P, OUT_GROUP, D], F32, name="last_acc", tag="dots")
+            elif i == first:
                 acc[first] = acc_ps.tile([P, OUT_GROUP, D], F32, name="acc")
             for g in range(PASSES):
                 nc.tensor.matmul_mx(
@@ -245,12 +263,13 @@ def tile_polynomialattn_kernel(tc, q, k, v, out):
             tiles = [it - PV_LAG - 1, it - PV_LAG]
             return [i for i in tiles if is_tile(i) and (i % OUT_GROUP == 0) == (i == tiles[0])]
 
-        def store(last, count):
+        def store(last, count, copy=nc.scalar.copy):
             h, r = divmod(last, ROW_TILES)
-            bank = acc[last - last % OUT_GROUP]
-            end = last % OUT_GROUP + 1
+            first = first_in_bank(last)
+            bank = acc[first]
+            end = last - first + 1
             result = work.tile([P, OUT_GROUP, D], F32, name="result")
-            nc.scalar.copy(out=result[:, :count, :], in_=bank[:, end - count : end, :])
+            copy(out=result[:, :count, :], in_=bank[:, end - count : end, :])
             rows = out_heads[h].rearrange("(p r) d -> p r d", r=ROW_TILES)
             nc.sync.dma_start(out=rows[:, r + 1 - count : r + 1, :], in_=result[:, :count, :])
 
@@ -258,16 +277,23 @@ def tile_polynomialattn_kernel(tc, q, k, v, out):
         for half in range(HALVES):
             blocks = range(half * ROW_TILES // HALVES, (half + 1) * ROW_TILES // HALVES)
             keep_keys(nc.scalar.copy, flip_rows(k_in[0], blocks), kT[0], blocks)
-            keep_queries(nc.vector.tensor_copy, flip_rows(q_in[0], blocks), qT[0], blocks)
+            if half == 0:
+                blocks = range(FIRST_SCORES)
+                keep_queries(nc.vector.tensor_copy, flip_rows(q_in[0], blocks), qT[0], blocks)
+        for i in range(FIRST_SCORES):
+            for half in range(HALVES):
+                score_matmul(i, half)
+        regroup_v(0)
+        quantise_v(0)
+        blocks = range(FIRST_SCORES, ROW_TILES)
+        keep_queries(nc.vector.tensor_copy, flip_rows(q_in[0], blocks), qT[0], blocks)
 
-        for h in range(V_AHEAD):
-            regroup_v(h)
-        for h in range(V_AHEAD):
-            quantise_v(h)
+        regroup_v(1)
+        quantise_v(1)
 
         flipped_rows = {}
         all_blocks = range(ROW_TILES)
-        for it in range(-1, N_TILES + STORE_LAG + 1):
+        for it in range(N_TILES + 1):
             next_head = it // ROW_TILES + 1
             at = it % ROW_TILES if is_tile(it) and next_head < HEADS else -1
             if next_head in EARLY_HEADS:
@@ -285,21 +311,15 @@ def tile_polynomialattn_kernel(tc, q, k, v, out):
             if at == PREPARE_Q_AT + 1:
                 qT[next_head] = new_turned("qT")
                 keep_queries(nc.scalar.copy, flipped_rows["q"], qT[next_head], all_blocks)
-            if is_tile(stored):
-                if stored >= N_TILES - OUT_GROUP:
-                    if stored == N_TILES - 2:
-                        store(stored, OUT_GROUP - 1)
-                    if stored == N_TILES - 1:
-                        store(stored, 1)
-                elif stored % OUT_GROUP == OUT_GROUP - 1:
-                    store(stored, OUT_GROUP)
+            if is_tile(stored) and stored % OUT_GROUP == OUT_GROUP - 1:
+                store(stored, OUT_GROUP)
             if is_tile(it - EVAC_LAG) and on_scalar(it - EVAC_LAG):
                 evacuate(it - EVAC_LAG)
             if is_tile(it):
                 square(it, 1)
 
             for half in range(HALVES):
-                if is_tile(it + 1):
+                if is_tile(it + 1) and it + 1 >= FIRST_SCORES:
                     score_matmul(it + 1, half)
             for half in range(HALVES):
                 if is_tile(it - FLIP_LAG):
@@ -338,3 +358,31 @@ def tile_polynomialattn_kernel(tc, q, k, v, out):
                 evacuate(it - EVAC_LAG)
             if m >= 0:
                 invert(m)
+
+        last = N_TILES - 1
+        store(last - 8, OUT_GROUP)
+        evacuate(last - 5)
+        flip(last - 4)
+        quantise(last - 6)
+        attn_times_v(last - 7)
+        attn_times_v(last - 6)
+        for i in range(last - 3, last):
+            normalise(i)
+        evacuate(last - 4)
+        normalise(last, on_vector=False)
+        for i in (last - 5, last - 4):
+            quantise(i)
+        for i in range(last - 3, last):
+            flip(i)
+            evacuate(i)
+        for i in (last - 5, last - 4):
+            attn_times_v(i)
+        flip(last)
+        evacuate(last)
+        store(last - 4, OUT_GROUP)
+        for i in range(last - 3, last + 1):
+            quantise(i)
+            attn_times_v(i)
+            if i == last - 1:
+                store(i, OUT_GROUP - 1)
+        store(last, 1, nc.vector.tensor_copy)

from contextlib import ExitStack

import concourse.mybir as mybir
from concourse.masks import make_identity

F32 = mybir.dt.float32
BF16 = mybir.dt.bfloat16
U32 = mybir.dt.uint32
U8 = mybir.dt.uint8
FP8X4 = mybir.dt.float8_e4m3fn_x4
COPY = mybir.ActivationFunctionType.Copy
SQUARE = mybir.ActivationFunctionType.Square
ADD = mybir.AluOpType.add
MAX = mybir.AluOpType.max
MULT = mybir.AluOpType.mult

P = 128
HEADS = 8
S = 1024
T = 1024
D = 128
EPS = 1e-4

ROW_TILES = S // P
N_TILES = HEADS * ROW_TILES
BANK = 512
HALVES = T // BANK
PACK = 4
K_PASS = P * PACK
PASSES = T // K_PASS
PAIRS = 2
OUT_GROUP = BANK // D
SUM_GROUP = 4

NORM_LAG = SUM_GROUP + 1
FLIP_LAG = NORM_LAG + 1
EVAC_LAG = FLIP_LAG + 1
QUANT_LAG = EVAC_LAG + 1
PV_LAG = QUANT_LAG + 1
STORE_LAG = PV_LAG + 1

PREPARE_K_AT = 2
PREPARE_Q_AT = 5

SCALAR_TILE = 3

EARLY_HEADS = [1, 2]

FIRST_SCORES = 2

V_AHEAD = 2
REGROUP_V_AT = 3
QUANTISE_V_AT = 4


FLOPS = 2 * 2 * HEADS * S * T * D


def tile_polynomialattn_kernel(tc, q, k, v, out):
    nc = tc.nc
    q_heads = q.rearrange("b h s d -> (b h) s d")
    k_heads = k.rearrange("b h t d -> (b h) t d")
    v_heads = v.rearrange("b h t d -> (b h) t d")
    out_heads = out.rearrange("b h s d -> (b h) s d")

    with ExitStack() as ctx:
        consts = ctx.enter_context(tc.tile_pool(name="consts", bufs=1))
        inputs = ctx.enter_context(tc.tile_pool(name="inputs", bufs=1))
        heads = ctx.enter_context(tc.tile_pool(name="heads", bufs=3))
        work = ctx.enter_context(tc.tile_pool(name="work", bufs=3))
        dots_ps = ctx.enter_context(tc.psum_pool(name="dots_ps", bufs=4))
        flip_ps = ctx.enter_context(tc.psum_pool(name="flip_ps", bufs=3))
        acc_ps = ctx.enter_context(tc.psum_pool(name="acc_ps", bufs=1))
        ctx.enter_context(tc.manual_schedule())

        q_in, k_in, v_in = {}, {}, {}

        def load_qk(h, pieces):
            k_in[h] = inputs.tile([P, ROW_TILES, D], BF16, name="k_in%d" % h)
            q_in[h] = inputs.tile([P, ROW_TILES, D], BF16, name="q_in%d" % h)
            k_rows = k_heads[h].rearrange("(r p) d -> p r d", p=P)
            q_rows = q_heads[h].rearrange("(p r) d -> p r d", r=ROW_TILES)
            for i in range(pieces):
                blocks = slice(i * ROW_TILES // pieces, (i + 1) * ROW_TILES // pieces)
                nc.sync.dma_start(out=k_in[h][:, blocks, :], in_=k_rows[:, blocks, :])
                nc.sync.dma_start(out=q_in[h][:, blocks, :], in_=q_rows[:, blocks, :])

        def load_v(h):
            v_in[h] = inputs.tile([P, PASSES * PACK, D], BF16, name="v_in%d" % h)
            nc.sync.dma_start(
                out=v_in[h][:].rearrange("p (g j) d -> p g j d", j=PACK),
                in_=v_heads[h].rearrange("(g p j) d -> p g j d", p=P, j=PACK),
            )

        load_qk(0, HALVES)
        load_v(0)
        load_qk(1, 1)
        load_v(1)
        load_qk(2, 1)
        for h in range(2, HEADS):
            load_v(h)
            if h + 1 < HEADS:
                load_qk(h + 1, 1)

        ident_bf = consts.tile([P, P], BF16, name="ident_bf")
        make_identity(nc, ident_bf[:])
        ident_f32 = consts.tile([P, P], F32, name="ident_f32")
        make_identity(nc, ident_f32[:])

        qT, kT, v_grouped, v_codes, v_scales = {}, {}, {}, {}, {}
        dots, x, rowsum, denom, rden, attn = {}, {}, {}, {}, {}, {}
        flipped, grouped, codes, scales, acc = {}, {}, {}, {}, {}

        def is_tile(i):
            return 0 <= i < N_TILES

        def flip_rows(rows, blocks):
            bank = flip_ps.tile([P, ROW_TILES, P], BF16, name="flip_rows", tag="flip")
            for r in blocks:
                nc.tensor.transpose(out=bank[:, r, :], in_=rows[:, r, :], identity=ident_bf[:])
            return bank

        def words_of(tile, blocks):
            width = P // 2
            return tile.bitcast(F32)[:, blocks[0] * width : (blocks[-1] + 1) * width]

        def keep_queries(copy, bank, turned, blocks):
            flat = bank[:].rearrange("d r p -> d (r p)")
            copy(out=words_of(turned[:], blocks), in_=words_of(flat, blocks))

        def keep_keys(copy, bank, turned, blocks):
            flat = bank[:].rearrange("d r p -> d (r p)")
            copy(
                out=words_of(turned[:], blocks).rearrange("d (g u p) -> d g u p", u=PAIRS, p=P),
                in_=words_of(flat, blocks).rearrange("d (g p u) -> d g u p", u=PAIRS, p=P),
            )

        def new_turned(name):
            return heads.tile([P, ROW_TILES * P], BF16, name=name)

        def regroup_v(h):
            v_grouped[h] = heads.tile([P, PASSES, D, PACK], BF16, name="v_grouped", align_bytes=64)
            nc.vector.tensor_copy(
                out=v_grouped[h][:], in_=v_in[h][:].rearrange("p (g j) d -> p g d j", j=PACK)
            )

        def quantise_v(h):
            v_codes[h] = inputs.tile([P, PASSES * D], U32, name="v_codes%d" % h, align_bytes=64)
            v_scales[h] = inputs.tile([P, PASSES * D], U8, name="v_scales%d" % h, align_bytes=64)
            nc.vector.quantize_mx(
                out=v_codes[h][:].bitcast(FP8X4),
                scales=v_scales[h][:],
                in_=v_grouped[h][:].rearrange("p g d j -> p (g d j)"),
            )

        def score_matmul(i, half):
            h, r = divmod(i, ROW_TILES)
            dots[i, half] = dots_ps.tile([P, BANK], F32, name="dots", tag="dots")
            nc.tensor.matmul(
                out=dots[i, half][:],
                lhsT=qT[h][:, r * P : (r + 1) * P],
                rhs=kT[h][:, half * BANK : (half + 1) * BANK],
                start=True,
                stop=True,
            )

        def square(i, half):
            m, j = divmod(i, SUM_GROUP)
            if half == 0:
                x[i] = work.tile([P, T], F32, name="x", bufs=NORM_LAG + 6)
            if half == 0 and j == 0:
                rowsum[m] = work.tile([P, SUM_GROUP, HALVES], F32, name="rowsum", bufs=5)
            nc.scalar.activation(
                out=x[i][:, half * BANK : (half + 1) * BANK],
                in_=dots[i, half][:],
                func=SQUARE,
                accum_out=rowsum[m][:, j, half : half + 1],
            )

        def add_sums(m):
            denom[m] = work.tile([P, SUM_GROUP], F32, name="denom")
            nc.vector.tensor_tensor(
                out=denom[m][:], in0=rowsum[m][:, :, 0], in1=rowsum[m][:, :, 1], op=ADD
            )

        def clamp(m):
            nc.vector.tensor_scalar(
                out=denom[m][:], in0=denom[m][:], scalar1=EPS, scalar2=None, op0=MAX
            )

        def invert(m):
            rden[m] = work.tile([P, SUM_GROUP], F32, name="rden")
            nc.vector.reciprocal(out=rden[m][:], in_=denom[m][:])

        def normalise(i, on_vector=True):
            m, j = divmod(i, SUM_GROUP)
            attn[i] = work.tile([P, T], BF16, name="attn", bufs=SUM_GROUP + 1)
            factor = rden[m][:, j : j + 1]
            if on_vector:
                nc.vector.tensor_scalar(
                    out=attn[i][:], in0=x[i][:], scalar1=factor, scalar2=None, op0=MULT
                )
            else:
                nc.scalar.activation(out=attn[i][:], in_=x[i][:], func=COPY, scale=factor)

        def flip_words(i, g):
            if g == 0:
                flipped[i] = flip_ps.tile([P, PASSES * PAIRS, P], F32, name="flipped", tag="flip")
            words = attn[i][:].bitcast(F32)
            for u in range(PAIRS):
                c = PAIRS * g + u
                nc.tensor.transpose(
                    out=flipped[i][:, c, :], in_=words[:, c * P : (c + 1) * P], identity=ident_f32[:]
                )

        def flip(i):
            for g in range(PASSES):
                flip_words(i, g)

        def on_scalar(i):
            if i == N_TILES - 2:
                return False
            return i % ROW_TILES == SCALAR_TILE or i + EVAC_LAG >= N_TILES

        def evacuate(i):
            grouped[i] = work.tile([P, PASSES * P * PACK], BF16, name="grouped", align_bytes=64)
            dst = grouped[i][:].bitcast(F32).rearrange("p (g s u) -> p g s u", g=PASSES, u=PAIRS)
            src = flipped[i][:].rearrange("p (g u) s -> p g s u", u=PAIRS)
            if on_scalar(i):
                nc.scalar.copy(out=dst, in_=src)
            else:
                nc.vector.tensor_copy(out=dst, in_=src)

        def quantise(i):
            codes[i] = work.tile([P, PASSES * P], U32, name="codes", align_bytes=64, bufs=4)
            scales[i] = work.tile([P, PASSES * P], U8, name="scales", align_bytes=64, bufs=4)
            nc.vector.quantize_mx(
                out=codes[i][:].bitcast(FP8X4), scales=scales[i][:], in_=grouped[i][:]
            )

        def first_in_bank(i):
            return i if i == N_TILES - 1 else i - i % OUT_GROUP

        def attn_times_v(i):
            h, r = divmod(i, ROW_TILES)
            first = first_in_bank(i)
            if i == first and i >= N_TILES - OUT_GROUP:
                acc[first] = dots_ps.tile([P, OUT_GROUP, D], F32, name="last_acc", tag="dots")
            elif i == first:
                acc[first] = acc_ps.tile([P, OUT_GROUP, D], F32, name="acc")
            for g in range(PASSES):
                nc.tensor.matmul_mx(
                    out=acc[first][:, i - first, :],
                    lhsT=codes[i][:, g * P : (g + 1) * P].bitcast(FP8X4),
                    lhsT_scale=scales[i][:, g * P : (g + 1) * P],
                    rhs=v_codes[h][:, g * D : (g + 1) * D].bitcast(FP8X4),
                    rhs_scale=v_scales[h][:, g * D : (g + 1) * D],
                    start=(g == 0),
                    stop=(g == PASSES - 1),
                )

        def multiplied_in(it):
            tiles = [it - PV_LAG - 1, it - PV_LAG]
            return [i for i in tiles if is_tile(i) and (i % OUT_GROUP == 0) == (i == tiles[0])]

        def store(last, count, copy=nc.scalar.copy):
            h, r = divmod(last, ROW_TILES)
            first = first_in_bank(last)
            bank = acc[first]
            end = last - first + 1
            result = work.tile([P, OUT_GROUP, D], F32, name="result")
            copy(out=result[:, :count, :], in_=bank[:, end - count : end, :])
            rows = out_heads[h].rearrange("(p r) d -> p r d", r=ROW_TILES)
            nc.sync.dma_start(out=rows[:, r + 1 - count : r + 1, :], in_=result[:, :count, :])

        kT[0], qT[0] = new_turned("kT"), new_turned("qT")
        for half in range(HALVES):
            blocks = range(half * ROW_TILES // HALVES, (half + 1) * ROW_TILES // HALVES)
            keep_keys(nc.scalar.copy, flip_rows(k_in[0], blocks), kT[0], blocks)
            if half == 0:
                blocks = range(FIRST_SCORES)
                keep_queries(nc.vector.tensor_copy, flip_rows(q_in[0], blocks), qT[0], blocks)
        for i in range(FIRST_SCORES):
            for half in range(HALVES):
                score_matmul(i, half)
        regroup_v(0)
        quantise_v(0)
        blocks = range(FIRST_SCORES, ROW_TILES)
        keep_queries(nc.vector.tensor_copy, flip_rows(q_in[0], blocks), qT[0], blocks)

        regroup_v(1)
        quantise_v(1)

        flipped_rows = {}
        all_blocks = range(ROW_TILES)
        for it in range(N_TILES + 1):
            next_head = it // ROW_TILES + 1
            at = it % ROW_TILES if is_tile(it) and next_head < HEADS else -1
            if next_head in EARLY_HEADS:
                at = -1
            v_head = it // ROW_TILES + V_AHEAD
            v_at = it % ROW_TILES if is_tile(it) and v_head < HEADS else -1
            m = it // SUM_GROUP - 1 if it % SUM_GROUP == 0 and 0 < it <= N_TILES else -1
            stored = it - STORE_LAG

            if is_tile(it):
                square(it, 0)
            if at == PREPARE_K_AT + 1:
                kT[next_head] = new_turned("kT")
                keep_keys(nc.scalar.copy, flipped_rows["k"], kT[next_head], all_blocks)
            if at == PREPARE_Q_AT + 1:
                qT[next_head] = new_turned("qT")
                keep_queries(nc.scalar.copy, flipped_rows["q"], qT[next_head], all_blocks)
            if is_tile(stored) and stored % OUT_GROUP == OUT_GROUP - 1:
                store(stored, OUT_GROUP)
            if is_tile(it - EVAC_LAG) and on_scalar(it - EVAC_LAG):
                evacuate(it - EVAC_LAG)
            if is_tile(it):
                square(it, 1)

            for half in range(HALVES):
                if is_tile(it + 1) and it + 1 >= FIRST_SCORES:
                    score_matmul(it + 1, half)
            for half in range(HALVES):
                if is_tile(it - FLIP_LAG):
                    flip_words(it - FLIP_LAG, half)
            if 0 <= it < 2 * len(EARLY_HEADS):
                rows = k_in if it % 2 == 0 else q_in
                flipped_rows[it] = flip_rows(rows[EARLY_HEADS[it // 2]], all_blocks)
            if at == PREPARE_K_AT:
                flipped_rows["k"] = flip_rows(k_in[next_head], all_blocks)
            if at == PREPARE_Q_AT:
                flipped_rows["q"] = flip_rows(q_in[next_head], all_blocks)
            for i in multiplied_in(it):
                attn_times_v(i)

            steps = [(normalise, it - NORM_LAG), (quantise, it - QUANT_LAG)]
            if it % SUM_GROUP == 1:
                steps.reverse()
            for n, (step, i) in enumerate(steps):
                if is_tile(i):
                    step(i)
                if m >= 0 and n == 0:
                    add_sums(m)
            if m >= 0:
                clamp(m)
            if v_at == REGROUP_V_AT:
                regroup_v(v_head)
            if v_at == QUANTISE_V_AT:
                quantise_v(v_head)
            early = it - 1
            if early in flipped_rows:
                h = EARLY_HEADS[early // 2]
                turned, keep = (kT, keep_keys) if early % 2 == 0 else (qT, keep_queries)
                turned[h] = new_turned("kT" if early % 2 == 0 else "qT")
                keep(nc.vector.tensor_copy, flipped_rows[early], turned[h], all_blocks)
            if is_tile(it - EVAC_LAG) and not on_scalar(it - EVAC_LAG):
                evacuate(it - EVAC_LAG)
            if m >= 0:
                invert(m)

        last = N_TILES - 1
        store(last - 8, OUT_GROUP)
        evacuate(last - 5)
        flip(last - 4)
        quantise(last - 6)
        attn_times_v(last - 7)
        attn_times_v(last - 6)
        for i in range(last - 3, last):
            normalise(i)
        evacuate(last - 4)
        normalise(last, on_vector=False)
        for i in (last - 5, last - 4):
            quantise(i)
        for i in range(last - 3, last):
            flip(i)
            evacuate(i)
        for i in (last - 5, last - 4):
            attn_times_v(i)
        flip(last)
        evacuate(last)
        store(last - 4, OUT_GROUP)
        for i in range(last - 3, last + 1):
            quantise(i)
            attn_times_v(i)
            if i == last - 1:
                store(i, OUT_GROUP - 1)
        store(last, 1, nc.vector.tensor_copy)
